import numpy as np
import ml_dtypes


def mxq(x, axis, fmt="e4m3"):
    dtype, down = {"e4m3": (ml_dtypes.float8_e4m3fn, 7), "e5m2": (ml_dtypes.float8_e5m2, 14)}[fmt]
    v = np.moveaxis(np.asarray(x, np.float32).astype(ml_dtypes.bfloat16).astype(np.float64), axis, -1)
    blocks = v.reshape(v.shape[:-1] + (-1, 32))
    amax = np.abs(blocks).max(-1, keepdims=True)
    byte = np.maximum(np.where(amax > 0, np.frexp(amax)[1] - 1 + 127, 0) - down, 1)
    scale = np.exp2(byte - 127.0)
    codes = (blocks / scale).astype(np.float32).astype(dtype).astype(np.float64)
    return np.moveaxis((codes * scale).reshape(v.shape), -1, axis)


WIDE = False


def mx_kscale(k):
    if not WIDE:
        return np.ones(k)
    levels = np.array([30, -30])
    if k % 512:
        return np.exp2(np.random.permutation(np.resize(levels, k // 32))).repeat(32)
    a = np.empty((k // 512, 16))
    for p in range(k // 512):
        a[p, :8] = np.random.permutation(np.resize(levels, 8))
        for g in range(8):
            far = levels[np.abs(levels - a[p, g]) >= 10]
            a[p, g + 8] = far[np.random.randint(len(far))]
    return np.exp2(a.ravel()).repeat(32)


BF16 = ml_dtypes.bfloat16


def bf(x):
    return np.asarray(x, np.float32).astype(BF16)


def f64(x):
    return np.asarray(x).astype(np.float64)


B, S, D, H = 4, 1024, 512, 4
DH = D // H
ROPE_BASE = 10000.0


def rope_split(x, freqs_cis):
    b, s, h, dh = x.shape
    xr = x.reshape(b, s, h, dh // 2, 2)
    x_real, x_imag = xr[..., 0], xr[..., 1]
    fc = freqs_cis[:s][:, None, :, :]
    cos, sin = fc[..., 0], fc[..., 1]
    rot_real = x_real * cos - x_imag * sin
    rot_imag = x_real * sin + x_imag * cos
    return np.concatenate([rot_real, rot_imag], axis=-1)


def setup_inputs():
    s = mx_kscale(D)
    inv_freq = 1.0 / ROPE_BASE ** (np.arange(0, DH, 2) / DH)
    ang = np.outer(np.arange(S), inv_freq)
    return {"hidden_states": bf(np.random.standard_normal((B, S, D)) * s),
            "freqs_cis": bf(np.stack([np.cos(ang), np.sin(ang)], axis=-1)),
            "Wq": bf(np.random.standard_normal((D, D)) / np.sqrt(D) / s),
            "bq": bf(np.random.standard_normal(D) * 0.3),
            "Wk": bf(np.random.standard_normal((D, D)) / np.sqrt(D) / s),
            "bk": bf(np.random.standard_normal(D) * 0.3)}


def reference(hidden_states, freqs_cis, Wq, bq, Wk, bk):
    x = f64(hidden_states)
    b, s, _ = x.shape
    fc = f64(freqs_cis)
    xq = mxq(x, 2, "e5m2")
    q = ((xq @ mxq(f64(Wq), 1, "e4m3").T) + f64(bq)).reshape(b, s, H, DH)
    k = ((xq @ mxq(f64(Wk), 1, "e4m3").T) + f64(bk)).reshape(b, s, H, DH)
    return rope_split(q, fc), rope_split(k, fc)

@@ -1,0 +1,296 @@
+from contextlib import ExitStack
+
+import concourse.mybir as mybir
+from concourse.masks import make_identity
+
+B, S, D, H = 4, 1024, 512, 4
+DH = D // H
+FLOPS = 2 * 2 * B * S * D * D
+
+F32 = mybir.dt.float32
+BF16 = mybir.dt.bfloat16
+U32 = mybir.dt.uint32
+U8 = mybir.dt.uint8
+E5M2X4 = mybir.dt.float8_e5m2_x4
+E4M3X4 = mybir.dt.float8_e4m3fn_x4
+ALU = mybir.AluOpType
+ACT = mybir.ActivationFunctionType
+
+P = 128
+GROUP = 512
+SUB = GROUP // P
+GROUPS = B * S // GROUP
+UNITS = 4
+LAGS = (1, 2, 2, 3)
+POOL_ADD = (1, 3)
+POOL_MUL = (2,)
+FIRST_LAGS = (1, 2, 2, 3)
+FIRST_ADD = (1, 3)
+FIRST_MUL = (2,)
+FIRST_QUANT = 1
+FIRST_TURN = (0, 0)
+FINE_FROM = 24
+TABLE_STEP = 8
+SPLIT_FROM = 31
+LAST_LAGS = (1, 2, 1, 1)
+LAST_ADD = (1,)
+LAST_MUL = ()
+QUANT_STEP = 1
+TURN_STEPS = (-1, 0)
+
+
+def pick(g, first, middle, last):
+    return first if g == 0 else last if g == GROUPS - 1 else middle
+
+
+def tile_attention_pa_t_kernel(tc, hidden_states, freqs_cis, Wq, bq, Wk, bk, out_0, out_1):
+    nc = tc.nc
+    x_rows = hidden_states.rearrange("b s k -> (b s) k")
+    out_rows = [o.rearrange("b s h d -> (b s) (h d)") for o in (out_0, out_1)]
+    weights = (Wq, Wk)
+    biases = (bq, bk)
+    halves = S // GROUP
+
+    def group_rows(g):
+        half, batch = divmod(g, B)
+        start = batch * S + half * GROUP
+        return slice(start, start + GROUP)
+
+    with ExitStack() as ctx:
+        keep = ctx.enter_context(tc.tile_pool(name="keep", bufs=1))
+        work = ctx.enter_context(tc.tile_pool(name="work", bufs=2))
+        prod = ctx.enter_context(tc.tile_pool(name="prod", bufs=4))
+        outp = ctx.enter_context(tc.tile_pool(name="outp", bufs=4))
+        mx_psum = ctx.enter_context(tc.psum_pool(name="mx_psum", bufs=4))
+        tr_psum = ctx.enter_context(tc.psum_pool(name="tr_psum", bufs=4))
+        ctx.enter_context(tc.manual_schedule())
+
+        ident = keep.tile([P, P], F32, name="ident")
+        make_identity(nc, ident[:])
+
+        w_raw = [keep.tile([P, 2, D], BF16, name="w_raw%d" % u) for u in range(UNITS)]
+        x_raw = [[keep.tile([P, 2, D], BF16, name="x_raw%d_%d" % (g, t)) for t in range(2)] for g in range(GROUPS)]
+        f_raw = [keep.tile([P, SUB, DH], BF16, name="f_raw%d" % h) for h in range(halves)]
+        bias = [keep.tile([P, 2, 2], BF16, name="bias%d" % i) for i in range(2)]
+        w_codes = [keep.tile([P, 2 * P], U32, name="w_codes%d" % u, align_bytes=64) for u in range(UNITS)]
+        w_scales = [keep.tile([P, 2 * P], U8, name="w_scales%d" % u, align_bytes=64) for u in range(UNITS)]
+        table = [keep.tile([P, 3, GROUP], F32, name="table%d" % h) for h in range(halves)]
+
+        def load_w(u):
+            qk, hp = divmod(u, 2)
+            rows = weights[qk][2 * P * hp : 2 * P * (hp + 1), :]
+            nc.sync.dma_start(out=w_raw[u][:], in_=rows.rearrange("(m e) k -> m e k", e=2))
+
+        def load_x(g):
+            rows = x_rows[group_rows(g), :].rearrange("(p q) k -> p q k", q=SUB)
+            for t in range(2):
+                nc.sync.dma_start(out=x_raw[g][t][:], in_=rows[:, 2 * t : 2 * t + 2, :])
+
+        def load_f(h):
+            rows = freqs_cis[h * GROUP : (h + 1) * GROUP].rearrange("(p q) j e -> p q (j e)", q=SUB)
+            nc.sync.dma_start(out=f_raw[h][:], in_=rows)
+
+        load_f(0)
+        load_w(0)
+        load_x(0)
+        for i in range(2):
+            nc.sync.dma_start(out=bias[i][:], in_=biases[i].rearrange("(hp m e) -> m hp e", hp=2, e=2))
+        for u in range(1, UNITS):
+            load_w(u)
+        load_x(1)
+        load_f(1)
+        for g in range(2, GROUPS):
+            load_x(g)
+
+        def turn_rows(src, dst):
+            bank = tr_psum.tile([P, 2, 2, P], F32, name="bank", tag="tr")
+            for r in range(2):
+                words = src[:, r, :].bitcast(F32)
+                for w in range(2):
+                    nc.tensor.transpose(bank[:, r, w, :], words[:, w : D // 2 : 2], ident[:])
+            return bank
+
+        def copy_turned(bank, dst):
+            nc.scalar.copy(
+                out=dst.bitcast(F32).rearrange("p (r n w) -> p r n w", r=2, w=2),
+                in_=bank[:].rearrange("p r w n -> p r n w"),
+            )
+
+        w_turned = {}
+
+        def turn_w(u):
+            w_turned[u] = work.tile([P, 2 * P * 4], BF16, name="w_turned", align_bytes=64, bufs=4)
+            copy_turned(turn_rows(w_raw[u], None), w_turned[u][:])
+
+        def quantize_w(u):
+            nc.vector.quantize_mx(out=w_codes[u][:].bitcast(E4M3X4), scales=w_scales[u][:], in_=w_turned[u][:])
+
+        x_turned, x_codes, x_scales = {}, {}, {}
+
+        def turn_x(g, part):
+            if part == 0:
+                x_turned[g] = work.tile([P, GROUP * 4], BF16, name="x_turned", align_bytes=64)
+            bank = turn_rows(x_raw[g][part], None)
+            copy_turned(bank, x_turned[g][:, part * GROUP * 2 : (part + 1) * GROUP * 2])
+
+        def quantize_x(g):
+            x_codes[g] = work.tile([P, GROUP], U32, name="x_codes", align_bytes=64)
+            x_scales[g] = work.tile([P, GROUP], U8, name="x_scales", align_bytes=64)
+            nc.vector.quantize_mx(out=x_codes[g][:].bitcast(E5M2X4), scales=x_scales[g][:], in_=x_turned[g][:])
+
+        spread = {}
+
+        def spread_angles(h):
+            spread[h] = work.tile([P, SUB, 2, DH // 2], F32, name="spread")
+            words = f_raw[h][:].bitcast(F32).unsqueeze(2).to_broadcast([P, SUB, 2, DH // 2])
+            if h == 0:
+                nc.vector.tensor_copy(out=spread[h][:], in_=words)
+            else:
+                nc.scalar.copy(out=spread[h][:], in_=words)
+
+        def make_table(h):
+            bank = tr_psum.tile([P, SUB, P], F32, name="bank", tag="tr")
+            for q in range(SUB):
+                nc.tensor.transpose(bank[:, q, :], spread[h][:, q].rearrange("p d j -> p (d j)"), ident[:])
+            pairs = bank[:].rearrange("p q n -> p (q n)").bitcast(BF16).rearrange("p (n e) -> p e n", e=2)
+            if h == 0:
+                nc.vector.tensor_copy(out=table[h][:, 1:3, :], in_=pairs)
+                nc.vector.tensor_scalar_mul(out=table[h][:, 0, :], in0=table[h][:, 2, :], scalar1=-1.0)
+            else:
+                nc.scalar.copy(out=table[h][:, 1:3, :], in_=pairs)
+                nc.scalar.mul(out=table[h][:, 0, :], in_=table[h][:, 2, :], mul=-1.0)
+
+        sums, terms = {}, {}
+
+        def project(i):
+            g, u = divmod(i, UNITS)
+            sums[i] = []
+            for e in range(2):
+                acc = mx_psum.tile([P, GROUP], F32, name="acc")
+                cols = slice(e * P, (e + 1) * P)
+                nc.tensor.matmul_mx(
+                    out=acc[:],
+                    lhsT=w_codes[u][:, cols].bitcast(E4M3X4),
+                    lhsT_scale=w_scales[u][:, cols],
+                    rhs=x_codes[g][:].bitcast(E5M2X4),
+                    rhs_scale=x_scales[g][:],
+                    start=True,
+                    stop=True,
+                )
+                sums[i].append(acc)
+
+        def multiply(i):
+            g, u = divmod(i, UNITS)
+            qk, hp = divmod(u, 2)
+            tab = table[g // B]
+            terms[i] = [prod.tile([P, 2, GROUP], F32, name="term%d" % e) for e in range(2)]
+            pieces = 2 if i >= SPLIT_FROM else 1
+            for piece in range(pieces):
+                cols = slice(piece * GROUP // pieces, (piece + 1) * GROUP // pieces)
+                for e in range(2):
+                    term = terms[i][e]
+                    factors = tab[:, 1 - e : 3 - e, cols]
+                    shift = bias[qk][:, hp, e : e + 1]
+                    if e == 1 and u in pick(g, FIRST_MUL, POOL_MUL, LAST_MUL):
+                        y = work.tile([P, GROUP // pieces], F32, name="y")
+                        nc.scalar.activation(out=y[:], in_=sums[i][e][:, cols], func=ACT.Identity, bias=shift)
+                        for r in range(2):
+                            nc.gpsimd.tensor_tensor(
+                                out=term[:, r, cols], in0=y[:], in1=factors[:, r, :], op=ALU.mult
+                            )
+                    else:
+                        nc.vector.scalar_tensor_tensor(
+                            out=term[:, :, cols],
+                            in0=sums[i][e][:, cols].unsqueeze(1).to_broadcast([P, 2, GROUP // pieces]),
+                            scalar=shift,
+                            in1=factors,
+                            op0=ALU.add,
+                            op1=ALU.mult,
+                        )
+            if u in pick(g, FIRST_ADD, POOL_ADD, LAST_ADD):
+                total = prod.tile([P, 2, GROUP], F32, name="total", bufs=3)
+                for r in range(2):
+                    nc.gpsimd.tensor_tensor(
+                        out=total[:, r, :], in0=terms[i][0][:, r, :], in1=terms[i][1][:, r, :], op=ALU.add
+                    )
+                terms[i] = [total]
+
+        rows_out = {}
+
+        def finish(i):
+            g, u = divmod(i, UNITS)
+            qk, hp = divmod(u, 2)
+            if hp == 0:
+                rows_out[g, qk] = outp.tile([P, SUB, D], F32, name="rows_out")
+            dst = rows_out[g, qk]
+            hbm = out_rows[qk][group_rows(g), :].rearrange("(p q) f -> p q f", q=SUB)
+            last = i == GROUPS * UNITS - 1
+            cols = slice(hp * 2 * DH, (hp + 1) * 2 * DH)
+            for part in range(2):
+                bank = tr_psum.tile([P, 2, 2, 2, DH // 2], F32, name="bank", tag="tr")
+                for qq in range(2):
+                    q = 2 * part + qq
+                    for r in range(2):
+                        n = len(terms[i])
+                        for t in range(n):
+                            nc.tensor.matmul(
+                                out=bank[:, qq, :, r, :],
+                                lhsT=terms[i][t][:, r, q * P : (q + 1) * P],
+                                rhs=ident[:],
+                                start=(t == 0),
+                                stop=(t == n - 1),
+                                is_transpose=True,
+                            )
+                nc.scalar.copy(
+                    out=dst[:, 2 * part : 2 * part + 2, cols],
+                    in_=bank[:].rearrange("p q h r j -> p q (h r j)"),
+                )
+                if last:
+                    nc.sync.dma_start(
+                        out=hbm[:, 2 * part : 2 * part + 2, cols], in_=dst[:, 2 * part : 2 * part + 2, cols]
+                    )
+            if last:
+                return
+            if i >= FINE_FROM:
+                nc.sync.dma_start(out=hbm[:, :, cols], in_=dst[:, :, cols])
+            elif hp == 1:
+                nc.sync.dma_start(out=hbm, in_=dst[:])
+
+        spread_angles(0)
+        turn_w(0)
+        make_table(0)
+        turn_x(0, 0)
+        turn_x(0, 1)
+        quantize_w(0)
+        quantize_x(0)
+        for u in range(1, UNITS):
+            turn_w(u)
+        project(0)
+        for u in range(1, UNITS):
+            quantize_w(u)
+        total_units = GROUPS * UNITS
+        finish_at = {}
+        for i in range(total_units):
+            g, u = divmod(i, UNITS)
+            finish_at.setdefault(i + pick(g, FIRST_LAGS, LAGS, LAST_LAGS)[u], []).append(i)
+        turn_at = {}
+        for g in range(1, GROUPS):
+            for part in range(2):
+                step = (g - 1) * UNITS + (FIRST_TURN if g == 1 else TURN_STEPS)[part]
+                turn_at.setdefault(step, []).append((g, part))
+        for i in range(max(finish_at) + 1):
+            g, u = divmod(i, UNITS)
+            if i + 1 < total_units:
+                project(i + 1)
+            for ahead, part in turn_at.get(i, []):
+                turn_x(ahead, part)
+            if i < total_units:
+                multiply(i)
+            if g + 1 < GROUPS and u == (FIRST_QUANT if g == 0 else QUANT_STEP):
+                quantize_x(g + 1)
+            if i == TABLE_STEP:
+                spread_angles(1)
+            if i == TABLE_STEP + 2:
+                make_table(1)
+            for done in finish_at.get(i, []):
+                finish(done)

@@ -21,16 +21,22 @@ GROUP = 512
 SUB = GROUP // P
 GROUPS = B * S // GROUP
 UNITS = 4
-LAGS = (1, 2, 2, 3)
+LAGS = (2, 3, 2, 4)
 POOL_ADD = (1, 3)
 POOL_MUL = (2,)
-FIRST_LAGS = (1, 2, 2, 3)
+FIRST_LAGS = (2, 3, 2, 4)
 FIRST_ADD = (1, 3)
 FIRST_MUL = (2,)
 FIRST_QUANT = 1
 FIRST_TURN = (0, 0)
 FINE_FROM = 24
 TABLE_STEP = 8
+PRE = False
+PRE_STEPS = (-2, -1)
+PIECES = 4
+HALF_ADD = ()
+MX_BUFS = 4
+PAIR = None
 SPLIT_FROM = 31
 LAST_LAGS = (1, 2, 1, 1)
 LAST_ADD = (1,)
@@ -39,8 +45,13 @@ QUANT_STEP = 1
 TURN_STEPS = (-1, 0)
 
 
-def pick(g, first, middle, last):
-    return first if g == 0 else last if g == GROUPS - 1 else middle
+PEN_ADD = (1, 3)
+PEN_MUL = (2,)
+PEN_LAGS = (2, 3, 2, 4)
+
+
+def pick(g, first, middle, last, pen):
+    return first if g == 0 else last if g == GROUPS - 1 else pen if g == GROUPS - 2 else middle
 
 
 def tile_attention_pa_t_kernel(tc, hidden_states, freqs_cis, Wq, bq, Wk, bk, out_0, out_1):
@@ -59,10 +70,10 @@ def tile_attention_pa_t_kernel(tc, hidden_states, freqs_cis, Wq, bq, Wk, bk, out
     with ExitStack() as ctx:
         keep = ctx.enter_context(tc.tile_pool(name="keep", bufs=1))
         work = ctx.enter_context(tc.tile_pool(name="work", bufs=2))
-        prod = ctx.enter_context(tc.tile_pool(name="prod", bufs=4))
+        prod = ctx.enter_context(tc.tile_pool(name="prod", bufs=6))
         outp = ctx.enter_context(tc.tile_pool(name="outp", bufs=4))
-        mx_psum = ctx.enter_context(tc.psum_pool(name="mx_psum", bufs=4))
-        tr_psum = ctx.enter_context(tc.psum_pool(name="tr_psum", bufs=4))
+        mx_psum = ctx.enter_context(tc.psum_pool(name="mx_psum", bufs=MX_BUFS))
+        tr_psum = ctx.enter_context(tc.psum_pool(name="tr_psum", bufs=8 - MX_BUFS))
         ctx.enter_context(tc.manual_schedule())
 
         ident = keep.tile([P, P], F32, name="ident")
@@ -127,16 +138,35 @@ def tile_attention_pa_t_kernel(tc, hidden_states, freqs_cis, Wq, bq, Wk, bk, out
 
         x_turned, x_codes, x_scales = {}, {}, {}
 
+        x_split = {}
+
+        def split_x(g, part):
+            x_split[g, part] = work.tile([P, 2, 2, P], F32, name="x_split", bufs=3)
+            words = x_raw[g][part][:].rearrange("p r k -> p (r k)").bitcast(F32)
+            nc.scalar.copy(out=x_split[g, part][:], in_=words.rearrange("p (r n w) -> p r w n", r=2, w=2))
+
         def turn_x(g, part):
             if part == 0:
                 x_turned[g] = work.tile([P, GROUP * 4], BF16, name="x_turned", align_bytes=64)
-            bank = turn_rows(x_raw[g][part], None)
+            if (g, part) in x_split:
+                bank = tr_psum.tile([P, 2, 2, P], F32, name="bank", tag="tr")
+                for r in range(2):
+                    for w in range(2):
+                        nc.tensor.transpose(bank[:, r, w, :], x_split[g, part][:, r, w, :], ident[:])
+            else:
+                bank = turn_rows(x_raw[g][part], None)
             copy_turned(bank, x_turned[g][:, part * GROUP * 2 : (part + 1) * GROUP * 2])
 
-        def quantize_x(g):
-            x_codes[g] = work.tile([P, GROUP], U32, name="x_codes", align_bytes=64)
-            x_scales[g] = work.tile([P, GROUP], U8, name="x_scales", align_bytes=64)
-            nc.vector.quantize_mx(out=x_codes[g][:].bitcast(E5M2X4), scales=x_scales[g][:], in_=x_turned[g][:])
+        def quantize_x(g, part=None):
+            if part in (None, 0):
+                x_codes[g] = work.tile([P, GROUP], U32, name="x_codes", align_bytes=64)
+                x_scales[g] = work.tile([P, GROUP], U8, name="x_scales", align_bytes=64)
+            lo, hi = (0, GROUP) if part is None else (part * GROUP // 2, (part + 1) * GROUP // 2)
+            nc.vector.quantize_mx(
+                out=x_codes[g][:, lo:hi].bitcast(E5M2X4),
+                scales=x_scales[g][:, lo:hi],
+                in_=x_turned[g][:, 4 * lo : 4 * hi],
+            )
 
         spread = {}
 
@@ -160,60 +190,87 @@ def tile_attention_pa_t_kernel(tc, hidden_states, freqs_cis, Wq, bq, Wk, bk, out
                 nc.scalar.copy(out=table[h][:, 1:3, :], in_=pairs)
                 nc.scalar.mul(out=table[h][:, 0, :], in_=table[h][:, 2, :], mul=-1.0)
 
-        sums, terms = {}, {}
+        sums, terms, shifted = {}, {}, {}
+
+        def mx(acc, i, e, cols):
+            g, u = divmod(i, UNITS)
+            rows = slice(e * P, (e + 1) * P)
+            nc.tensor.matmul_mx(
+                out=acc,
+                lhsT=w_codes[u][:, rows].bitcast(E4M3X4),
+                lhsT_scale=w_scales[u][:, rows],
+                rhs=x_codes[g][:, cols].bitcast(E5M2X4),
+                rhs_scale=x_scales[g][:, cols],
+                start=True,
+                stop=True,
+            )
+
+        def on_pool(i):
+            g, u = divmod(i, UNITS)
+            return u in pick(g, FIRST_MUL, POOL_MUL, LAST_MUL, PEN_MUL)
 
         def project(i):
             g, u = divmod(i, UNITS)
+            qk, hp = divmod(u, 2)
             sums[i] = []
             for e in range(2):
                 acc = mx_psum.tile([P, GROUP], F32, name="acc")
-                cols = slice(e * P, (e + 1) * P)
-                nc.tensor.matmul_mx(
-                    out=acc[:],
-                    lhsT=w_codes[u][:, cols].bitcast(E4M3X4),
-                    lhsT_scale=w_scales[u][:, cols],
-                    rhs=x_codes[g][:].bitcast(E5M2X4),
-                    rhs_scale=x_scales[g][:],
-                    start=True,
-                    stop=True,
-                )
+                mx(acc[:], i, e, slice(0, GROUP))
                 sums[i].append(acc)
+            if on_pool(i):
+                shifted[i] = work.tile([P, GROUP], F32, name="shifted")
+                nc.scalar.activation(
+                    out=shifted[i][:], in_=sums[i][1][:], func=ACT.Identity, bias=bias[qk][:, hp, 1:2]
+                )
+
+        def project_half(i, part):
+            acc = mx_psum.tile([P, 2, GROUP // 2], F32, name="acc")
+            cols = slice(part * GROUP // 2, (part + 1) * GROUP // 2)
+            for e in range(2):
+                mx(acc[:, e, :], i, e, cols)
+            return acc
+
+        def products(i, e, acc, cols):
+            g, u = divmod(i, UNITS)
+            qk, hp = divmod(u, 2)
+            nc.vector.scalar_tensor_tensor(
+                out=terms[i][e][:, :, cols],
+                in0=acc.unsqueeze(1).to_broadcast([P, 2, cols.stop - cols.start]),
+                scalar=bias[qk][:, hp, e : e + 1],
+                in1=table[g // B][:, 1 - e : 3 - e, cols],
+                op0=ALU.add,
+                op1=ALU.mult,
+            )
+
+        def new_terms(i):
+            terms[i] = [prod.tile([P, 2, GROUP], F32, name="term%d" % e) for e in range(2)]
 
         def multiply(i):
             g, u = divmod(i, UNITS)
-            qk, hp = divmod(u, 2)
-            tab = table[g // B]
-            terms[i] = [prod.tile([P, 2, GROUP], F32, name="term%d" % e) for e in range(2)]
-            pieces = 2 if i >= SPLIT_FROM else 1
+            new_terms(i)
+            pieces = PIECES if i >= SPLIT_FROM else 1
             for piece in range(pieces):
                 cols = slice(piece * GROUP // pieces, (piece + 1) * GROUP // pieces)
-                for e in range(2):
-                    term = terms[i][e]
-                    factors = tab[:, 1 - e : 3 - e, cols]
-                    shift = bias[qk][:, hp, e : e + 1]
-                    if e == 1 and u in pick(g, FIRST_MUL, POOL_MUL, LAST_MUL):
-                        y = work.tile([P, GROUP // pieces], F32, name="y")
-                        nc.scalar.activation(out=y[:], in_=sums[i][e][:, cols], func=ACT.Identity, bias=shift)
-                        for r in range(2):
-                            nc.gpsimd.tensor_tensor(
-                                out=term[:, r, cols], in0=y[:], in1=factors[:, r, :], op=ALU.mult
-                            )
-                    else:
-                        nc.vector.scalar_tensor_tensor(
-                            out=term[:, :, cols],
-                            in0=sums[i][e][:, cols].unsqueeze(1).to_broadcast([P, 2, GROUP // pieces]),
-                            scalar=shift,
-                            in1=factors,
-                            op0=ALU.add,
-                            op1=ALU.mult,
-                        )
-            if u in pick(g, FIRST_ADD, POOL_ADD, LAST_ADD):
-                total = prod.tile([P, 2, GROUP], F32, name="total", bufs=3)
-                for r in range(2):
-                    nc.gpsimd.tensor_tensor(
-                        out=total[:, r, :], in0=terms[i][0][:, r, :], in1=terms[i][1][:, r, :], op=ALU.add
-                    )
-                terms[i] = [total]
+                for e in range(1 if on_pool(i) else 2):
+                    products(i, e, sums[i][e][:, cols], cols)
+            if on_pool(i):
+                nc.gpsimd.tensor_tensor(
+                    out=terms[i][1][:],
+                    in0=shifted[i][:].unsqueeze(1).to_broadcast([P, 2, GROUP]),
+                    in1=table[g // B][:, 0:2, :],
+                    op=ALU.mult,
+                )
+
+        def combine(i):
+            g, u = divmod(i, UNITS)
+            even, odd = terms[i]
+            terms[i] = [[even[:, r, :], odd[:, r, :]] for r in range(2)]
+            if u in pick(g, FIRST_ADD, POOL_ADD, LAST_ADD, PEN_ADD):
+                total = prod.tile([P, 2, GROUP], F32, name="total", bufs=4)
+                n = 1 if u in HALF_ADD else 2
+                nc.gpsimd.tensor_tensor(out=total[:, :n, :], in0=even[:, :n, :], in1=odd[:, :n, :], op=ALU.add)
+                for r in range(n):
+                    terms[i][r] = [total[:, r, :]]
 
         rows_out = {}
 
@@ -226,29 +283,27 @@ def tile_attention_pa_t_kernel(tc, hidden_states, freqs_cis, Wq, bq, Wk, bk, out
             hbm = out_rows[qk][group_rows(g), :].rearrange("(p q) f -> p q f", q=SUB)
             last = i == GROUPS * UNITS - 1
             cols = slice(hp * 2 * DH, (hp + 1) * 2 * DH)
-            for part in range(2):
-                bank = tr_psum.tile([P, 2, 2, 2, DH // 2], F32, name="bank", tag="tr")
-                for qq in range(2):
-                    q = 2 * part + qq
+            parts = PIECES if last else 2
+            per = SUB // parts
+            for part in range(parts):
+                bank = tr_psum.tile([P, per, 2, 2, DH // 2], F32, name="bank", tag="tr")
+                for qq in range(per):
+                    q = per * part + qq
                     for r in range(2):
-                        n = len(terms[i])
+                        n = len(terms[i][r])
                         for t in range(n):
                             nc.tensor.matmul(
                                 out=bank[:, qq, :, r, :],
-                                lhsT=terms[i][t][:, r, q * P : (q + 1) * P],
+                                lhsT=terms[i][r][t][:, q * P : (q + 1) * P],
                                 rhs=ident[:],
                                 start=(t == 0),
                                 stop=(t == n - 1),
                                 is_transpose=True,
                             )
-                nc.scalar.copy(
-                    out=dst[:, 2 * part : 2 * part + 2, cols],
-                    in_=bank[:].rearrange("p q h r j -> p q (h r j)"),
-                )
+                subs = slice(per * part, per * (part + 1))
+                nc.scalar.copy(out=dst[:, subs, cols], in_=bank[:].rearrange("p q h r j -> p q (h r j)"))
                 if last:
-                    nc.sync.dma_start(
-                        out=hbm[:, 2 * part : 2 * part + 2, cols], in_=dst[:, 2 * part : 2 * part + 2, cols]
-                    )
+                    nc.sync.dma_start(out=hbm[:, subs, cols], in_=dst[:, subs, cols])
             if last:
                 return
             if i >= FINE_FROM:
@@ -257,35 +312,58 @@ def tile_attention_pa_t_kernel(tc, hidden_states, freqs_cis, Wq, bq, Wk, bk, out
                 nc.sync.dma_start(out=hbm, in_=dst[:])
 
         spread_angles(0)
-        turn_w(0)
         make_table(0)
+        turn_w(0)
         turn_x(0, 0)
-        turn_x(0, 1)
         quantize_w(0)
-        quantize_x(0)
-        for u in range(1, UNITS):
+        quantize_x(0, 0)
+        turn_x(0, 1)
+        turn_w(1)
+        first = project_half(0, 0)
+        quantize_x(0, 1)
+        quantize_w(1)
+        new_terms(0)
+        for e in range(2):
+            products(0, e, first[:, e, :], slice(0, GROUP // 2))
+        second = project_half(0, 1)
+        for u in range(2, UNITS):
             turn_w(u)
-        project(0)
-        for u in range(1, UNITS):
-            quantize_w(u)
+        for e in range(2):
+            products(0, e, second[:, e, :], slice(GROUP // 2, GROUP))
         total_units = GROUPS * UNITS
         finish_at = {}
         for i in range(total_units):
             g, u = divmod(i, UNITS)
-            finish_at.setdefault(i + pick(g, FIRST_LAGS, LAGS, LAST_LAGS)[u], []).append(i)
+            finish_at.setdefault(i + pick(g, FIRST_LAGS, LAGS, LAST_LAGS, PEN_LAGS)[u], []).append(i)
         turn_at = {}
+        split_at = {}
+        for g in range(2, GROUPS if PRE else 0):
+            for part in range(2):
+                split_at.setdefault((g - 1) * UNITS + PRE_STEPS[part], []).append((g, part))
         for g in range(1, GROUPS):
             for part in range(2):
                 step = (g - 1) * UNITS + (FIRST_TURN if g == 1 else TURN_STEPS)[part]
                 turn_at.setdefault(step, []).append((g, part))
         for i in range(max(finish_at) + 1):
             g, u = divmod(i, UNITS)
-            if i + 1 < total_units:
-                project(i + 1)
+            if PAIR is None or i == 0 and PAIR == 1:
+                if i + 1 < total_units:
+                    project(i + 1)
+            elif i % 2 == PAIR:
+                for j in (i + 1, i + 2):
+                    if j < total_units:
+                        project(j)
+            for ahead, part in split_at.get(i, []):
+                split_x(ahead, part)
             for ahead, part in turn_at.get(i, []):
                 turn_x(ahead, part)
-            if i < total_units:
+            if 0 < i < total_units:
                 multiply(i)
+            if i < total_units:
+                combine(i)
+            if i == 0:
+                for w in range(2, UNITS):
+                    quantize_w(w)
             if g + 1 < GROUPS and u == (FIRST_QUANT if g == 0 else QUANT_STEP):
                 quantize_x(g + 1)
             if i == TABLE_STEP:

@@ -17,47 +17,35 @@ ALU = mybir.AluOpType
 ACT = mybir.ActivationFunctionType
 
 P = 128
+PACK = 4
 GROUP = 512
-SUB = GROUP // P
+HALF = GROUP // 2
+SLOTS = GROUP // P
 GROUPS = B * S // GROUP
 UNITS = 4
-LAGS = (2, 3, 2, 4)
-POOL_ADD = (1, 3)
-POOL_MUL = (2,)
-FIRST_LAGS = (2, 3, 2, 4)
-FIRST_ADD = (1, 3)
-FIRST_MUL = (2,)
-FIRST_QUANT = 1
-FIRST_TURN = (0, 0)
-FINE_FROM = 24
-TABLE_STEP = 8
-PRE = False
-PRE_STEPS = (-2, -1)
-PIECES = 4
-HALF_ADD = ()
-MX_BUFS = 4
-PAIR = None
-SPLIT_FROM = 31
-LAST_LAGS = (1, 2, 1, 1)
-LAST_ADD = (1,)
-LAST_MUL = ()
-QUANT_STEP = 1
-TURN_STEPS = (-1, 0)
+LAST_UNIT = GROUPS * UNITS - 1
+LAG = 2
+
+POOL_PRODUCTS = (2,)
+POOL_SUMS = (1, 3)
+FIRST_POOL_PRODUCTS = (1, 2)
+FIRST_POOL_SUMS = (3,)
+LAST_POOL_PRODUCTS = ()
+LAST_POOL_SUMS = (1,)
+QUANTIZE_AFTER = 1
+FIRST_QUANTIZE_AFTER = 2
+SECOND_TABLE_STEP = 8
+DIRECT_GROUPS = 2
 
 
-PEN_ADD = (1, 3)
-PEN_MUL = (2,)
-PEN_LAGS = (2, 3, 2, 4)
-
-
-def pick(g, first, middle, last, pen):
-    return first if g == 0 else last if g == GROUPS - 1 else pen if g == GROUPS - 2 else middle
+def by_group(g, first, middle, last):
+    return first if g == 0 else last if g == GROUPS - 1 else middle
 
 
 def tile_attention_pa_t_kernel(tc, hidden_states, freqs_cis, Wq, bq, Wk, bk, out_0, out_1):
     nc = tc.nc
     x_rows = hidden_states.rearrange("b s k -> (b s) k")
-    out_rows = [o.rearrange("b s h d -> (b s) (h d)") for o in (out_0, out_1)]
+    out_rows = [out.rearrange("b s h d -> (b s) (h d)") for out in (out_0, out_1)]
     weights = (Wq, Wk)
     biases = (bq, bk)
     halves = S // GROUP
@@ -70,10 +58,10 @@ def tile_attention_pa_t_kernel(tc, hidden_states, freqs_cis, Wq, bq, Wk, bk, out
     with ExitStack() as ctx:
         keep = ctx.enter_context(tc.tile_pool(name="keep", bufs=1))
         work = ctx.enter_context(tc.tile_pool(name="work", bufs=2))
-        prod = ctx.enter_context(tc.tile_pool(name="prod", bufs=6))
-        outp = ctx.enter_context(tc.tile_pool(name="outp", bufs=4))
-        mx_psum = ctx.enter_context(tc.psum_pool(name="mx_psum", bufs=MX_BUFS))
-        tr_psum = ctx.enter_context(tc.psum_pool(name="tr_psum", bufs=8 - MX_BUFS))
+        prod = ctx.enter_context(tc.tile_pool(name="prod", bufs=LAG + 4))
+        result = ctx.enter_context(tc.tile_pool(name="result", bufs=8))
+        mx_psum = ctx.enter_context(tc.psum_pool(name="mx_psum", bufs=4))
+        tr_psum = ctx.enter_context(tc.psum_pool(name="tr_psum", bufs=4))
         ctx.enter_context(tc.manual_schedule())
 
         ident = keep.tile([P, P], F32, name="ident")
@@ -81,64 +69,61 @@ def tile_attention_pa_t_kernel(tc, hidden_states, freqs_cis, Wq, bq, Wk, bk, out
 
         w_raw = [keep.tile([P, 2, D], BF16, name="w_raw%d" % u) for u in range(UNITS)]
         x_raw = [[keep.tile([P, 2, D], BF16, name="x_raw%d_%d" % (g, t)) for t in range(2)] for g in range(GROUPS)]
-        f_raw = [keep.tile([P, SUB, DH], BF16, name="f_raw%d" % h) for h in range(halves)]
-        bias = [keep.tile([P, 2, 2], BF16, name="bias%d" % i) for i in range(2)]
+        angle_raw = [keep.tile([P, SLOTS, DH], BF16, name="angle_raw%d" % h) for h in range(halves)]
+        bias = [keep.tile([P, 2, 2], BF16, name="bias%d" % qk) for qk in range(2)]
         w_codes = [keep.tile([P, 2 * P], U32, name="w_codes%d" % u, align_bytes=64) for u in range(UNITS)]
         w_scales = [keep.tile([P, 2 * P], U8, name="w_scales%d" % u, align_bytes=64) for u in range(UNITS)]
         table = [keep.tile([P, 3, GROUP], F32, name="table%d" % h) for h in range(halves)]
 
         def load_w(u):
-            qk, hp = divmod(u, 2)
-            rows = weights[qk][2 * P * hp : 2 * P * (hp + 1), :]
+            qk, pair = divmod(u, 2)
+            rows = weights[qk][2 * P * pair : 2 * P * (pair + 1), :]
             nc.sync.dma_start(out=w_raw[u][:], in_=rows.rearrange("(m e) k -> m e k", e=2))
 
         def load_x(g):
-            rows = x_rows[group_rows(g), :].rearrange("(p q) k -> p q k", q=SUB)
-            for t in range(2):
-                nc.sync.dma_start(out=x_raw[g][t][:], in_=rows[:, 2 * t : 2 * t + 2, :])
+            rows = x_rows[group_rows(g), :].rearrange("(p q) k -> p q k", q=SLOTS)
+            for part in range(2):
+                nc.sync.dma_start(out=x_raw[g][part][:], in_=rows[:, 2 * part : 2 * part + 2, :])
 
-        def load_f(h):
-            rows = freqs_cis[h * GROUP : (h + 1) * GROUP].rearrange("(p q) j e -> p q (j e)", q=SUB)
-            nc.sync.dma_start(out=f_raw[h][:], in_=rows)
+        def load_angles(h):
+            rows = freqs_cis[h * GROUP : (h + 1) * GROUP].rearrange("(p q) j e -> p q (j e)", q=SLOTS)
+            nc.sync.dma_start(out=angle_raw[h][:], in_=rows)
 
-        load_f(0)
+        load_angles(0)
         load_w(0)
         load_x(0)
-        for i in range(2):
-            nc.sync.dma_start(out=bias[i][:], in_=biases[i].rearrange("(hp m e) -> m hp e", hp=2, e=2))
+        for qk in range(2):
+            nc.sync.dma_start(out=bias[qk][:], in_=biases[qk].rearrange("(pair m e) -> m pair e", pair=2, e=2))
         for u in range(1, UNITS):
             load_w(u)
         load_x(1)
-        load_f(1)
+        load_angles(1)
         for g in range(2, GROUPS):
             load_x(g)
 
-        def turn_rows(src, dst):
+        def turn(words, dst):
             bank = tr_psum.tile([P, 2, 2, P], F32, name="bank", tag="tr")
             for r in range(2):
-                words = src[:, r, :].bitcast(F32)
                 for w in range(2):
-                    nc.tensor.transpose(bank[:, r, w, :], words[:, w : D // 2 : 2], ident[:])
-            return bank
-
-        def copy_turned(bank, dst):
+                    nc.tensor.transpose(bank[:, r, w, :], words(r, w), ident[:])
             nc.scalar.copy(
                 out=dst.bitcast(F32).rearrange("p (r n w) -> p r n w", r=2, w=2),
                 in_=bank[:].rearrange("p r w n -> p r n w"),
             )
 
+        def every_second_word(raw):
+            return lambda r, w: raw[:, r, :].bitcast(F32)[:, w : D // 2 : 2]
+
         w_turned = {}
 
         def turn_w(u):
-            w_turned[u] = work.tile([P, 2 * P * 4], BF16, name="w_turned", align_bytes=64, bufs=4)
-            copy_turned(turn_rows(w_raw[u], None), w_turned[u][:])
+            w_turned[u] = work.tile([P, 2 * P * PACK], BF16, name="w_turned", align_bytes=64, bufs=UNITS)
+            turn(every_second_word(w_raw[u]), w_turned[u][:])
 
         def quantize_w(u):
             nc.vector.quantize_mx(out=w_codes[u][:].bitcast(E4M3X4), scales=w_scales[u][:], in_=w_turned[u][:])
 
-        x_turned, x_codes, x_scales = {}, {}, {}
-
-        x_split = {}
+        x_split, x_turned, x_codes, x_scales = {}, {}, {}, {}
 
         def split_x(g, part):
             x_split[g, part] = work.tile([P, 2, 2, P], F32, name="x_split", bufs=3)
@@ -147,228 +132,187 @@ def tile_attention_pa_t_kernel(tc, hidden_states, freqs_cis, Wq, bq, Wk, bk, out
 
         def turn_x(g, part):
             if part == 0:
-                x_turned[g] = work.tile([P, GROUP * 4], BF16, name="x_turned", align_bytes=64)
-            if (g, part) in x_split:
-                bank = tr_psum.tile([P, 2, 2, P], F32, name="bank", tag="tr")
-                for r in range(2):
-                    for w in range(2):
-                        nc.tensor.transpose(bank[:, r, w, :], x_split[g, part][:, r, w, :], ident[:])
+                x_turned[g] = work.tile([P, GROUP * PACK], BF16, name="x_turned", align_bytes=64)
+            dst = x_turned[g][:, part * HALF * PACK : (part + 1) * HALF * PACK]
+            if g < DIRECT_GROUPS:
+                turn(every_second_word(x_raw[g][part]), dst)
             else:
-                bank = turn_rows(x_raw[g][part], None)
-            copy_turned(bank, x_turned[g][:, part * GROUP * 2 : (part + 1) * GROUP * 2])
+                turn(lambda r, w: x_split[g, part][:, r, w, :], dst)
 
-        def quantize_x(g, part=None):
-            if part in (None, 0):
+        def quantize_x(g, cols):
+            if cols.start == 0:
                 x_codes[g] = work.tile([P, GROUP], U32, name="x_codes", align_bytes=64)
                 x_scales[g] = work.tile([P, GROUP], U8, name="x_scales", align_bytes=64)
-            lo, hi = (0, GROUP) if part is None else (part * GROUP // 2, (part + 1) * GROUP // 2)
             nc.vector.quantize_mx(
-                out=x_codes[g][:, lo:hi].bitcast(E5M2X4),
-                scales=x_scales[g][:, lo:hi],
-                in_=x_turned[g][:, 4 * lo : 4 * hi],
+                out=x_codes[g][:, cols].bitcast(E5M2X4),
+                scales=x_scales[g][:, cols],
+                in_=x_turned[g][:, PACK * cols.start : PACK * cols.stop],
             )
 
-        spread = {}
+        angle_twice = {}
 
-        def spread_angles(h):
-            spread[h] = work.tile([P, SUB, 2, DH // 2], F32, name="spread")
-            words = f_raw[h][:].bitcast(F32).unsqueeze(2).to_broadcast([P, SUB, 2, DH // 2])
-            if h == 0:
-                nc.vector.tensor_copy(out=spread[h][:], in_=words)
-            else:
-                nc.scalar.copy(out=spread[h][:], in_=words)
+        def repeat_angles(h, copy):
+            angle_twice[h] = work.tile([P, SLOTS, 2, DH // 2], F32, name="angle_twice")
+            words = angle_raw[h][:].bitcast(F32).unsqueeze(2).to_broadcast([P, SLOTS, 2, DH // 2])
+            copy(out=angle_twice[h][:], in_=words)
 
-        def make_table(h):
-            bank = tr_psum.tile([P, SUB, P], F32, name="bank", tag="tr")
-            for q in range(SUB):
-                nc.tensor.transpose(bank[:, q, :], spread[h][:, q].rearrange("p d j -> p (d j)"), ident[:])
+        def turn_angles(h, copy):
+            bank = tr_psum.tile([P, SLOTS, P], F32, name="bank", tag="tr")
+            for q in range(SLOTS):
+                nc.tensor.transpose(bank[:, q, :], angle_twice[h][:, q].rearrange("p d j -> p (d j)"), ident[:])
             pairs = bank[:].rearrange("p q n -> p (q n)").bitcast(BF16).rearrange("p (n e) -> p e n", e=2)
-            if h == 0:
-                nc.vector.tensor_copy(out=table[h][:, 1:3, :], in_=pairs)
-                nc.vector.tensor_scalar_mul(out=table[h][:, 0, :], in0=table[h][:, 2, :], scalar1=-1.0)
-            else:
-                nc.scalar.copy(out=table[h][:, 1:3, :], in_=pairs)
-                nc.scalar.mul(out=table[h][:, 0, :], in_=table[h][:, 2, :], mul=-1.0)
+            copy(out=table[h][:, 1:3, :], in_=pairs)
 
-        sums, terms, shifted = {}, {}, {}
+        sums, shifted, terms, addends = {}, {}, {}, {}
 
-        def mx(acc, i, e, cols):
+        def pool_products(i):
             g, u = divmod(i, UNITS)
-            rows = slice(e * P, (e + 1) * P)
+            return u in by_group(g, FIRST_POOL_PRODUCTS, POOL_PRODUCTS, LAST_POOL_PRODUCTS)
+
+        def pool_sums(i):
+            g, u = divmod(i, UNITS)
+            return u in by_group(g, FIRST_POOL_SUMS, POOL_SUMS, LAST_POOL_SUMS)
+
+        def unit_bias(i, e):
+            qk, pair = divmod(i % UNITS, 2)
+            return bias[qk][:, pair, e : e + 1]
+
+        def matmul(acc, i, e, cols):
+            g, u = divmod(i, UNITS)
+            features = slice(e * P, (e + 1) * P)
             nc.tensor.matmul_mx(
                 out=acc,
-                lhsT=w_codes[u][:, rows].bitcast(E4M3X4),
-                lhsT_scale=w_scales[u][:, rows],
+                lhsT=w_codes[u][:, features].bitcast(E4M3X4),
+                lhsT_scale=w_scales[u][:, features],
                 rhs=x_codes[g][:, cols].bitcast(E5M2X4),
                 rhs_scale=x_scales[g][:, cols],
                 start=True,
                 stop=True,
             )
 
-        def on_pool(i):
-            g, u = divmod(i, UNITS)
-            return u in pick(g, FIRST_MUL, POOL_MUL, LAST_MUL, PEN_MUL)
-
         def project(i):
-            g, u = divmod(i, UNITS)
-            qk, hp = divmod(u, 2)
             sums[i] = []
             for e in range(2):
                 acc = mx_psum.tile([P, GROUP], F32, name="acc")
-                mx(acc[:], i, e, slice(0, GROUP))
+                matmul(acc[:], i, e, slice(0, GROUP))
                 sums[i].append(acc)
-            if on_pool(i):
+            if pool_products(i):
                 shifted[i] = work.tile([P, GROUP], F32, name="shifted")
-                nc.scalar.activation(
-                    out=shifted[i][:], in_=sums[i][1][:], func=ACT.Identity, bias=bias[qk][:, hp, 1:2]
-                )
+                nc.scalar.activation(out=shifted[i][:], in_=sums[i][1][:], func=ACT.Identity, bias=unit_bias(i, 1))
 
-        def project_half(i, part):
-            acc = mx_psum.tile([P, 2, GROUP // 2], F32, name="acc")
-            cols = slice(part * GROUP // 2, (part + 1) * GROUP // 2)
+        def project_half(i, cols):
+            acc = mx_psum.tile([P, 2, HALF], F32, name="acc")
             for e in range(2):
-                mx(acc[:, e, :], i, e, cols)
+                matmul(acc[:, e, :], i, e, cols)
             return acc
-
-        def products(i, e, acc, cols):
-            g, u = divmod(i, UNITS)
-            qk, hp = divmod(u, 2)
-            nc.vector.scalar_tensor_tensor(
-                out=terms[i][e][:, :, cols],
-                in0=acc.unsqueeze(1).to_broadcast([P, 2, cols.stop - cols.start]),
-                scalar=bias[qk][:, hp, e : e + 1],
-                in1=table[g // B][:, 1 - e : 3 - e, cols],
-                op0=ALU.add,
-                op1=ALU.mult,
-            )
 
         def new_terms(i):
             terms[i] = [prod.tile([P, 2, GROUP], F32, name="term%d" % e) for e in range(2)]
 
+        def vector_products(i, e, acc, cols):
+            nc.vector.scalar_tensor_tensor(
+                out=terms[i][e][:, :, cols],
+                in0=acc.unsqueeze(1).to_broadcast([P, 2, cols.stop - cols.start]),
+                scalar=unit_bias(i, e),
+                in1=table[i // UNITS // B][:, 1 - e : 3 - e, cols],
+                op0=ALU.add,
+                op1=ALU.mult,
+            )
+
         def multiply(i):
-            g, u = divmod(i, UNITS)
             new_terms(i)
-            pieces = PIECES if i >= SPLIT_FROM else 1
-            for piece in range(pieces):
-                cols = slice(piece * GROUP // pieces, (piece + 1) * GROUP // pieces)
-                for e in range(1 if on_pool(i) else 2):
-                    products(i, e, sums[i][e][:, cols], cols)
-            if on_pool(i):
+            width = P if i == LAST_UNIT else GROUP
+            for start in range(0, GROUP, width):
+                cols = slice(start, start + width)
+                for e in range(1 if pool_products(i) else 2):
+                    vector_products(i, e, sums[i][e][:, cols], cols)
+            if pool_products(i):
                 nc.gpsimd.tensor_tensor(
                     out=terms[i][1][:],
                     in0=shifted[i][:].unsqueeze(1).to_broadcast([P, 2, GROUP]),
-                    in1=table[g // B][:, 0:2, :],
+                    in1=table[i // UNITS // B][:, 0:2, :],
                     op=ALU.mult,
                 )
 
         def combine(i):
-            g, u = divmod(i, UNITS)
-            even, odd = terms[i]
-            terms[i] = [[even[:, r, :], odd[:, r, :]] for r in range(2)]
-            if u in pick(g, FIRST_ADD, POOL_ADD, LAST_ADD, PEN_ADD):
-                total = prod.tile([P, 2, GROUP], F32, name="total", bufs=4)
-                n = 1 if u in HALF_ADD else 2
-                nc.gpsimd.tensor_tensor(out=total[:, :n, :], in0=even[:, :n, :], in1=odd[:, :n, :], op=ALU.add)
-                for r in range(n):
-                    terms[i][r] = [total[:, r, :]]
-
-        rows_out = {}
+            addends[i] = terms[i]
+            if pool_sums(i):
+                total = prod.tile([P, 2, GROUP], F32, name="total", bufs=LAG + 2)
+                nc.gpsimd.tensor_tensor(out=total[:], in0=terms[i][0][:], in1=terms[i][1][:], op=ALU.add)
+                addends[i] = [total]
 
         def finish(i):
             g, u = divmod(i, UNITS)
-            qk, hp = divmod(u, 2)
-            if hp == 0:
-                rows_out[g, qk] = outp.tile([P, SUB, D], F32, name="rows_out")
-            dst = rows_out[g, qk]
-            hbm = out_rows[qk][group_rows(g), :].rearrange("(p q) f -> p q f", q=SUB)
-            last = i == GROUPS * UNITS - 1
-            cols = slice(hp * 2 * DH, (hp + 1) * 2 * DH)
-            parts = PIECES if last else 2
-            per = SUB // parts
-            for part in range(parts):
-                bank = tr_psum.tile([P, per, 2, 2, DH // 2], F32, name="bank", tag="tr")
-                for qq in range(per):
-                    q = per * part + qq
+            qk, pair = divmod(u, 2)
+            hbm = out_rows[qk][group_rows(g), pair * 2 * DH : (pair + 1) * 2 * DH]
+            hbm = hbm.rearrange("(p q) f -> p q f", q=SLOTS)
+            per_bank = 1 if i == LAST_UNIT else 2
+            for first in range(0, SLOTS, per_bank):
+                bank = tr_psum.tile([P, per_bank, 2, 2, DH // 2], F32, name="bank", tag="tr")
+                for q in range(first, first + per_bank):
                     for r in range(2):
-                        n = len(terms[i][r])
-                        for t in range(n):
+                        for t, addend in enumerate(addends[i]):
                             nc.tensor.matmul(
-                                out=bank[:, qq, :, r, :],
-                                lhsT=terms[i][r][t][:, q * P : (q + 1) * P],
+                                out=bank[:, q - first, :, r, :],
+                                lhsT=addend[:, r, q * P : (q + 1) * P],
                                 rhs=ident[:],
                                 start=(t == 0),
-                                stop=(t == n - 1),
+                                stop=(t == len(addends[i]) - 1),
                                 is_transpose=True,
                             )
-                subs = slice(per * part, per * (part + 1))
-                nc.scalar.copy(out=dst[:, subs, cols], in_=bank[:].rearrange("p q h r j -> p q (h r j)"))
-                if last:
-                    nc.sync.dma_start(out=hbm[:, subs, cols], in_=dst[:, subs, cols])
-            if last:
-                return
-            if i >= FINE_FROM:
-                nc.sync.dma_start(out=hbm[:, :, cols], in_=dst[:, :, cols])
-            elif hp == 1:
-                nc.sync.dma_start(out=hbm, in_=dst[:])
+                rows = result.tile([P, per_bank, 2 * DH], F32, name="rows")
+                nc.scalar.copy(out=rows[:], in_=bank[:].rearrange("p q h r j -> p q (h r j)"))
+                nc.sync.dma_start(out=hbm[:, first : first + per_bank, :], in_=rows[:])
 
-        spread_angles(0)
-        make_table(0)
+        low, high = slice(0, HALF), slice(HALF, GROUP)
+        repeat_angles(0, nc.vector.tensor_copy)
+        turn_angles(0, nc.vector.tensor_copy)
+        nc.vector.tensor_scalar_mul(out=table[0][:, 0, :], in0=table[0][:, 2, :], scalar1=-1.0)
         turn_w(0)
         turn_x(0, 0)
         quantize_w(0)
-        quantize_x(0, 0)
+        quantize_x(0, low)
         turn_x(0, 1)
         turn_w(1)
-        first = project_half(0, 0)
-        quantize_x(0, 1)
+        acc_low = project_half(0, low)
+        quantize_x(0, high)
         quantize_w(1)
         new_terms(0)
         for e in range(2):
-            products(0, e, first[:, e, :], slice(0, GROUP // 2))
-        second = project_half(0, 1)
+            vector_products(0, e, acc_low[:, e, :], low)
+        acc_high = project_half(0, high)
         for u in range(2, UNITS):
             turn_w(u)
         for e in range(2):
-            products(0, e, second[:, e, :], slice(GROUP // 2, GROUP))
-        total_units = GROUPS * UNITS
-        finish_at = {}
-        for i in range(total_units):
+            vector_products(0, e, acc_high[:, e, :], high)
+
+        for i in range(LAST_UNIT + LAG + 1):
             g, u = divmod(i, UNITS)
-            finish_at.setdefault(i + pick(g, FIRST_LAGS, LAGS, LAST_LAGS, PEN_LAGS)[u], []).append(i)
-        turn_at = {}
-        split_at = {}
-        for g in range(2, GROUPS if PRE else 0):
+            if i < LAST_UNIT:
+                project(i + 1)
             for part in range(2):
-                split_at.setdefault((g - 1) * UNITS + PRE_STEPS[part], []).append((g, part))
-        for g in range(1, GROUPS):
+                ahead, rest = divmod(i + 2 - part, UNITS)
+                if rest == 0 and DIRECT_GROUPS <= ahead + 1 < GROUPS:
+                    split_x(ahead + 1, part)
             for part in range(2):
-                step = (g - 1) * UNITS + (FIRST_TURN if g == 1 else TURN_STEPS)[part]
-                turn_at.setdefault(step, []).append((g, part))
-        for i in range(max(finish_at) + 1):
-            g, u = divmod(i, UNITS)
-            if PAIR is None or i == 0 and PAIR == 1:
-                if i + 1 < total_units:
-                    project(i + 1)
-            elif i % 2 == PAIR:
-                for j in (i + 1, i + 2):
-                    if j < total_units:
-                        project(j)
-            for ahead, part in split_at.get(i, []):
-                split_x(ahead, part)
-            for ahead, part in turn_at.get(i, []):
-                turn_x(ahead, part)
-            if 0 < i < total_units:
+                ahead, rest = divmod(i + 1 - part, UNITS)
+                if i == 0:
+                    turn_x(1, part)
+                elif rest == 0 and ahead + 1 < GROUPS:
+                    turn_x(ahead + 1, part)
+            if 0 < i <= LAST_UNIT:
                 multiply(i)
-            if i < total_units:
+            if i <= LAST_UNIT:
                 combine(i)
             if i == 0:
-                for w in range(2, UNITS):
-                    quantize_w(w)
-            if g + 1 < GROUPS and u == (FIRST_QUANT if g == 0 else QUANT_STEP):
-                quantize_x(g + 1)
-            if i == TABLE_STEP:
-                spread_angles(1)
-            if i == TABLE_STEP + 2:
-                make_table(1)
-            for done in finish_at.get(i, []):
-                finish(done)
+                for later in range(2, UNITS):
+                    quantize_w(later)
+            if g + 1 < GROUPS and u == (FIRST_QUANTIZE_AFTER if g == 0 else QUANTIZE_AFTER):
+                quantize_x(g + 1, slice(0, GROUP))
+            if i == SECOND_TABLE_STEP:
+                repeat_angles(1, nc.scalar.copy)
+            if i == SECOND_TABLE_STEP + 2:
+                turn_angles(1, nc.scalar.copy)
+                nc.scalar.mul(out=table[1][:, 0, :], in_=table[1][:, 2, :], mul=-1.0)
+            if i >= LAG:
+                finish(i - LAG)

@@ -26,12 +26,14 @@ UNITS = 4
 LAST_UNIT = GROUPS * UNITS - 1
 LAG = 2
 
-POOL_PRODUCTS = (2,)
-POOL_SUMS = (1, 3)
-FIRST_POOL_PRODUCTS = (1, 2)
-FIRST_POOL_SUMS = (3,)
-LAST_POOL_PRODUCTS = ()
-LAST_POOL_SUMS = (1,)
+PARTIAL_PRODUCTS = 1
+PARTIAL_SUMS = 3
+POOL_PRODUCTS = (PARTIAL_PRODUCTS, 0, SLOTS, 0)
+POOL_SUMS = (0, PARTIAL_SUMS, 0, SLOTS)
+FIRST_POOL_PRODUCTS = (0, SLOTS, SLOTS, 0)
+FIRST_POOL_SUMS = (0, 0, 0, SLOTS)
+LAST_POOL_PRODUCTS = POOL_PRODUCTS[:2] + (0, 0)
+LAST_POOL_SUMS = POOL_SUMS[:2] + (0, 0)
 QUANTIZE_AFTER = 1
 FIRST_QUANTIZE_AFTER = 2
 SECOND_TABLE_STEP = 8
@@ -71,8 +73,9 @@ def tile_attention_pa_t_kernel(tc, hidden_states, freqs_cis, Wq, bq, Wk, bk, out
         x_raw = [[keep.tile([P, 2, D], BF16, name="x_raw%d_%d" % (g, t)) for t in range(2)] for g in range(GROUPS)]
         angle_raw = [keep.tile([P, SLOTS, DH], BF16, name="angle_raw%d" % h) for h in range(halves)]
         bias = [keep.tile([P, 2, 2], BF16, name="bias%d" % qk) for qk in range(2)]
-        w_codes = [keep.tile([P, 2 * P], U32, name="w_codes%d" % u, align_bytes=64) for u in range(UNITS)]
-        w_scales = [keep.tile([P, 2 * P], U8, name="w_scales%d" % u, align_bytes=64) for u in range(UNITS)]
+        w_turned = keep.tile([P, UNITS, 2 * P * PACK], BF16, name="w_turned", align_bytes=64)
+        w_codes = keep.tile([P, UNITS, 2 * P], U32, name="w_codes", align_bytes=64)
+        w_scales = keep.tile([P, UNITS, 2 * P], U8, name="w_scales", align_bytes=64)
         table = [keep.tile([P, 3, GROUP], F32, name="table%d" % h) for h in range(halves)]
 
         def load_w(u):
@@ -114,14 +117,15 @@ def tile_attention_pa_t_kernel(tc, hidden_states, freqs_cis, Wq, bq, Wk, bk, out
         def every_second_word(raw):
             return lambda r, w: raw[:, r, :].bitcast(F32)[:, w : D // 2 : 2]
 
-        w_turned = {}
-
         def turn_w(u):
-            w_turned[u] = work.tile([P, 2 * P * PACK], BF16, name="w_turned", align_bytes=64, bufs=UNITS)
-            turn(every_second_word(w_raw[u]), w_turned[u][:])
+            turn(every_second_word(w_raw[u]), w_turned[:, u, :])
 
-        def quantize_w(u):
-            nc.vector.quantize_mx(out=w_codes[u][:].bitcast(E4M3X4), scales=w_scales[u][:], in_=w_turned[u][:])
+        def quantize_w(units):
+            nc.vector.quantize_mx(
+                out=w_codes[:, units, :].rearrange("p u c -> p (u c)").bitcast(E4M3X4),
+                scales=w_scales[:, units, :].rearrange("p u c -> p (u c)"),
+                in_=w_turned[:, units, :].rearrange("p u c -> p (u c)"),
+            )
 
         x_split, x_turned, x_codes, x_scales = {}, {}, {}, {}
 
@@ -167,11 +171,11 @@ def tile_attention_pa_t_kernel(tc, hidden_states, freqs_cis, Wq, bq, Wk, bk, out
 
         def pool_products(i):
             g, u = divmod(i, UNITS)
-            return u in by_group(g, FIRST_POOL_PRODUCTS, POOL_PRODUCTS, LAST_POOL_PRODUCTS)
+            return P * by_group(g, FIRST_POOL_PRODUCTS, POOL_PRODUCTS, LAST_POOL_PRODUCTS)[u]
 
         def pool_sums(i):
             g, u = divmod(i, UNITS)
-            return u in by_group(g, FIRST_POOL_SUMS, POOL_SUMS, LAST_POOL_SUMS)
+            return P * by_group(g, FIRST_POOL_SUMS, POOL_SUMS, LAST_POOL_SUMS)[u]
 
         def unit_bias(i, e):
             qk, pair = divmod(i % UNITS, 2)
@@ -182,8 +186,8 @@ def tile_attention_pa_t_kernel(tc, hidden_states, freqs_cis, Wq, bq, Wk, bk, out
             features = slice(e * P, (e + 1) * P)
             nc.tensor.matmul_mx(
                 out=acc,
-                lhsT=w_codes[u][:, features].bitcast(E4M3X4),
-                lhsT_scale=w_scales[u][:, features],
+                lhsT=w_codes[:, u, features].bitcast(E4M3X4),
+                lhsT_scale=w_scales[:, u, features],
                 rhs=x_codes[g][:, cols].bitcast(E5M2X4),
                 rhs_scale=x_scales[g][:, cols],
                 start=True,
@@ -196,9 +200,10 @@ def tile_attention_pa_t_kernel(tc, hidden_states, freqs_cis, Wq, bq, Wk, bk, out
                 acc = mx_psum.tile([P, GROUP], F32, name="acc")
                 matmul(acc[:], i, e, slice(0, GROUP))
                 sums[i].append(acc)
-            if pool_products(i):
-                shifted[i] = work.tile([P, GROUP], F32, name="shifted")
-                nc.scalar.activation(out=shifted[i][:], in_=sums[i][1][:], func=ACT.Identity, bias=unit_bias(i, 1))
+            n = pool_products(i)
+            if n:
+                shifted[i] = work.tile([P, n], F32, name="shifted")
+                nc.scalar.activation(out=shifted[i][:], in_=sums[i][1][:, :n], func=ACT.Identity, bias=unit_bias(i, 1))
 
         def project_half(i, cols):
             acc = mx_psum.tile([P, 2, HALF], F32, name="acc")
@@ -222,24 +227,29 @@ def tile_attention_pa_t_kernel(tc, hidden_states, freqs_cis, Wq, bq, Wk, bk, out
         def multiply(i):
             new_terms(i)
             width = P if i == LAST_UNIT else GROUP
+            n = pool_products(i)
             for start in range(0, GROUP, width):
-                cols = slice(start, start + width)
-                for e in range(1 if pool_products(i) else 2):
-                    vector_products(i, e, sums[i][e][:, cols], cols)
-            if pool_products(i):
+                vector_products(i, 0, sums[i][0][:, start : start + width], slice(start, start + width))
+                if n < start + width:
+                    cols = slice(max(n, start), start + width)
+                    vector_products(i, 1, sums[i][1][:, cols], cols)
+            if n:
                 nc.gpsimd.tensor_tensor(
-                    out=terms[i][1][:],
-                    in0=shifted[i][:].unsqueeze(1).to_broadcast([P, 2, GROUP]),
-                    in1=table[i // UNITS // B][:, 0:2, :],
+                    out=terms[i][1][:, :, :n],
+                    in0=shifted[i][:].unsqueeze(1).to_broadcast([P, 2, n]),
+                    in1=table[i // UNITS // B][:, 0:2, :n],
                     op=ALU.mult,
                 )
 
         def combine(i):
-            addends[i] = terms[i]
-            if pool_sums(i):
-                total = prod.tile([P, 2, GROUP], F32, name="total", bufs=LAG + 2)
-                nc.gpsimd.tensor_tensor(out=total[:], in0=terms[i][0][:], in1=terms[i][1][:], op=ALU.add)
-                addends[i] = [total]
+            addends[i] = [terms[i]] * SLOTS
+            n = pool_sums(i)
+            if n:
+                total = prod.tile([P, 2, n], F32, name="total", bufs=LAG + 2)
+                nc.gpsimd.tensor_tensor(
+                    out=total[:], in0=terms[i][0][:, :, :n], in1=terms[i][1][:, :, :n], op=ALU.add
+                )
+                addends[i] = [[total] if q * P < n else terms[i] for q in range(SLOTS)]
 
         def finish(i):
             g, u = divmod(i, UNITS)
@@ -251,13 +261,13 @@ def tile_attention_pa_t_kernel(tc, hidden_states, freqs_cis, Wq, bq, Wk, bk, out
                 bank = tr_psum.tile([P, per_bank, 2, 2, DH // 2], F32, name="bank", tag="tr")
                 for q in range(first, first + per_bank):
                     for r in range(2):
-                        for t, addend in enumerate(addends[i]):
+                        for t, addend in enumerate(addends[i][q]):
                             nc.tensor.matmul(
                                 out=bank[:, q - first, :, r, :],
                                 lhsT=addend[:, r, q * P : (q + 1) * P],
                                 rhs=ident[:],
                                 start=(t == 0),
-                                stop=(t == len(addends[i]) - 1),
+                                stop=(t == len(addends[i][q]) - 1),
                                 is_transpose=True,
                             )
                 rows = result.tile([P, per_bank, 2 * DH], F32, name="rows")
@@ -270,21 +280,22 @@ def tile_attention_pa_t_kernel(tc, hidden_states, freqs_cis, Wq, bq, Wk, bk, out
         nc.vector.tensor_scalar_mul(out=table[0][:, 0, :], in0=table[0][:, 2, :], scalar1=-1.0)
         turn_w(0)
         turn_x(0, 0)
-        quantize_w(0)
+        quantize_w(slice(0, 1))
         quantize_x(0, low)
         turn_x(0, 1)
         turn_w(1)
         acc_low = project_half(0, low)
         quantize_x(0, high)
-        quantize_w(1)
-        new_terms(0)
-        for e in range(2):
-            vector_products(0, e, acc_low[:, e, :], low)
         acc_high = project_half(0, high)
         for u in range(2, UNITS):
             turn_w(u)
+        new_terms(0)
+        for e in range(2):
+            vector_products(0, e, acc_low[:, e, :], low)
+        quantize_w(slice(1, 2))
         for e in range(2):
             vector_products(0, e, acc_high[:, e, :], high)
+        quantize_w(slice(2, UNITS))
 
         for i in range(LAST_UNIT + LAG + 1):
             g, u = divmod(i, UNITS)
@@ -304,9 +315,6 @@ def tile_attention_pa_t_kernel(tc, hidden_states, freqs_cis, Wq, bq, Wk, bk, out
                 multiply(i)
             if i <= LAST_UNIT:
                 combine(i)
-            if i == 0:
-                for later in range(2, UNITS):
-                    quantize_w(later)
             if g + 1 < GROUPS and u == (FIRST_QUANTIZE_AFTER if g == 0 else QUANTIZE_AFTER):
                 quantize_x(g + 1, slice(0, GROUP))
             if i == SECOND_TABLE_STEP:

@@ -37,6 +37,7 @@ LAST_POOL_SUMS = POOL_SUMS[:2] + (0, 0)
 QUANTIZE_AFTER = 1
 FIRST_QUANTIZE_AFTER = 2
 SECOND_TABLE_STEP = 8
+WARM_UPS = 5
 DIRECT_GROUPS = 2
 
 
@@ -274,6 +275,16 @@ def tile_attention_pa_t_kernel(tc, hidden_states, freqs_cis, Wq, bq, Wk, bk, out
                 nc.scalar.copy(out=rows[:], in_=bank[:].rearrange("p q h r j -> p q (h r j)"))
                 nc.sync.dma_start(out=hbm[:, first : first + per_bank, :], in_=rows[:])
 
+        zeros = keep.tile([P, GROUP], BF16, name="zeros")
+        unread = mx_psum.tile([P, GROUP], F32, name="unread", tag="acc")
+        nc.vector.memset(zeros[:], 0.0)
+
+        def warm_up():
+            nc.tensor.matmul(out=unread[:], lhsT=zeros[:, :P], rhs=zeros[:], start=True, stop=True)
+
+        for step in range(WARM_UPS):
+            warm_up()
+
         low, high = slice(0, HALF), slice(HALF, GROUP)
         repeat_angles(0, nc.vector.tensor_copy)
         turn_angles(0, nc.vector.tensor_copy)
@@ -283,6 +294,7 @@ def tile_attention_pa_t_kernel(tc, hidden_states, freqs_cis, Wq, bq, Wk, bk, out
         quantize_w(slice(0, 1))
         quantize_x(0, low)
         turn_x(0, 1)
+        warm_up()
         turn_w(1)
         acc_low = project_half(0, low)
         quantize_x(0, high)

from contextlib import ExitStack

import concourse.mybir as mybir
from concourse.masks import make_identity

B, S, D, H = 4, 1024, 512, 4
DH = D // H
FLOPS = 2 * 2 * B * S * D * D

F32 = mybir.dt.float32
BF16 = mybir.dt.bfloat16
U32 = mybir.dt.uint32
U8 = mybir.dt.uint8
E5M2X4 = mybir.dt.float8_e5m2_x4
E4M3X4 = mybir.dt.float8_e4m3fn_x4
ALU = mybir.AluOpType
ACT = mybir.ActivationFunctionType

P = 128
PACK = 4
GROUP = 512
HALF = GROUP // 2
SLOTS = GROUP // P
GROUPS = B * S // GROUP
UNITS = 4
LAST_UNIT = GROUPS * UNITS - 1
LAG = 2

PARTIAL_PRODUCTS = 1
PARTIAL_SUMS = 3
POOL_PRODUCTS = (PARTIAL_PRODUCTS, 0, SLOTS, 0)
POOL_SUMS = (0, PARTIAL_SUMS, 0, SLOTS)
FIRST_POOL_PRODUCTS = (0, SLOTS, SLOTS, 0)
FIRST_POOL_SUMS = (0, 0, 0, SLOTS)
LAST_POOL_PRODUCTS = POOL_PRODUCTS[:2] + (0, 0)
LAST_POOL_SUMS = POOL_SUMS[:2] + (0, 0)
QUANTIZE_AFTER = 1
FIRST_QUANTIZE_AFTER = 2
SECOND_TABLE_STEP = 8
WARM_UPS = 5
DIRECT_GROUPS = 2


def by_group(g, first, middle, last):
    return first if g == 0 else last if g == GROUPS - 1 else middle


def tile_attention_pa_t_kernel(tc, hidden_states, freqs_cis, Wq, bq, Wk, bk, out_0, out_1):
    nc = tc.nc
    x_rows = hidden_states.rearrange("b s k -> (b s) k")
    out_rows = [out.rearrange("b s h d -> (b s) (h d)") for out in (out_0, out_1)]
    weights = (Wq, Wk)
    biases = (bq, bk)
    halves = S // GROUP

    def group_rows(g):
        half, batch = divmod(g, B)
        start = batch * S + half * GROUP
        return slice(start, start + GROUP)

    with ExitStack() as ctx:
        keep = ctx.enter_context(tc.tile_pool(name="keep", bufs=1))
        work = ctx.enter_context(tc.tile_pool(name="work", bufs=2))
        prod = ctx.enter_context(tc.tile_pool(name="prod", bufs=LAG + 4))
        result = ctx.enter_context(tc.tile_pool(name="result", bufs=8))
        mx_psum = ctx.enter_context(tc.psum_pool(name="mx_psum", bufs=4))
        tr_psum = ctx.enter_context(tc.psum_pool(name="tr_psum", bufs=4))
        ctx.enter_context(tc.manual_schedule())

        ident = keep.tile([P, P], F32, name="ident")
        make_identity(nc, ident[:])

        w_raw = [keep.tile([P, 2, D], BF16, name="w_raw%d" % u) for u in range(UNITS)]
        x_raw = [[keep.tile([P, 2, D], BF16, name="x_raw%d_%d" % (g, t)) for t in range(2)] for g in range(GROUPS)]
        angle_raw = [keep.tile([P, SLOTS, DH], BF16, name="angle_raw%d" % h) for h in range(halves)]
        bias = [keep.tile([P, 2, 2], BF16, name="bias%d" % qk) for qk in range(2)]
        w_turned = keep.tile([P, UNITS, 2 * P * PACK], BF16, name="w_turned", align_bytes=64)
        w_codes = keep.tile([P, UNITS, 2 * P], U32, name="w_codes", align_bytes=64)
        w_scales = keep.tile([P, UNITS, 2 * P], U8, name="w_scales", align_bytes=64)
        table = [keep.tile([P, 3, GROUP], F32, name="table%d" % h) for h in range(halves)]

        def load_w(u):
            qk, pair = divmod(u, 2)
            rows = weights[qk][2 * P * pair : 2 * P * (pair + 1), :]
            nc.sync.dma_start(out=w_raw[u][:], in_=rows.rearrange("(m e) k -> m e k", e=2))

        def load_x(g):
            rows = x_rows[group_rows(g), :].rearrange("(p q) k -> p q k", q=SLOTS)
            for part in range(2):
                nc.sync.dma_start(out=x_raw[g][part][:], in_=rows[:, 2 * part : 2 * part + 2, :])

        def load_angles(h):
            rows = freqs_cis[h * GROUP : (h + 1) * GROUP].rearrange("(p q) j e -> p q (j e)", q=SLOTS)
            nc.sync.dma_start(out=angle_raw[h][:], in_=rows)

        load_angles(0)
        load_w(0)
        load_x(0)
        for qk in range(2):
            nc.sync.dma_start(out=bias[qk][:], in_=biases[qk].rearrange("(pair m e) -> m pair e", pair=2, e=2))
        for u in range(1, UNITS):
            load_w(u)
        load_x(1)
        load_angles(1)
        for g in range(2, GROUPS):
            load_x(g)

        def turn(words, dst):
            bank = tr_psum.tile([P, 2, 2, P], F32, name="bank", tag="tr")
            for r in range(2):
                for w in range(2):
                    nc.tensor.transpose(bank[:, r, w, :], words(r, w), ident[:])
            nc.scalar.copy(
                out=dst.bitcast(F32).rearrange("p (r n w) -> p r n w", r=2, w=2),
                in_=bank[:].rearrange("p r w n -> p r n w"),
            )

        def every_second_word(raw):
            return lambda r, w: raw[:, r, :].bitcast(F32)[:, w : D // 2 : 2]

        def turn_w(u):
            turn(every_second_word(w_raw[u]), w_turned[:, u, :])

        def quantize_w(units):
            nc.vector.quantize_mx(
                out=w_codes[:, units, :].rearrange("p u c -> p (u c)").bitcast(E4M3X4),
                scales=w_scales[:, units, :].rearrange("p u c -> p (u c)"),
                in_=w_turned[:, units, :].rearrange("p u c -> p (u c)"),
            )

        x_split, x_turned, x_codes, x_scales = {}, {}, {}, {}

        def split_x(g, part):
            x_split[g, part] = work.tile([P, 2, 2, P], F32, name="x_split", bufs=3)
            words = x_raw[g][part][:].rearrange("p r k -> p (r k)").bitcast(F32)
            nc.scalar.copy(out=x_split[g, part][:], in_=words.rearrange("p (r n w) -> p r w n", r=2, w=2))

        def turn_x(g, part):
            if part == 0:
                x_turned[g] = work.tile([P, GROUP * PACK], BF16, name="x_turned", align_bytes=64)
            dst = x_turned[g][:, part * HALF * PACK : (part + 1) * HALF * PACK]
            if g < DIRECT_GROUPS:
                turn(every_second_word(x_raw[g][part]), dst)
            else:
                turn(lambda r, w: x_split[g, part][:, r, w, :], dst)

        def quantize_x(g, cols):
            if cols.start == 0:
                x_codes[g] = work.tile([P, GROUP], U32, name="x_codes", align_bytes=64)
                x_scales[g] = work.tile([P, GROUP], U8, name="x_scales", align_bytes=64)
            nc.vector.quantize_mx(
                out=x_codes[g][:, cols].bitcast(E5M2X4),
                scales=x_scales[g][:, cols],
                in_=x_turned[g][:, PACK * cols.start : PACK * cols.stop],
            )

        angle_twice = {}

        def repeat_angles(h, copy):
            angle_twice[h] = work.tile([P, SLOTS, 2, DH // 2], F32, name="angle_twice")
            words = angle_raw[h][:].bitcast(F32).unsqueeze(2).to_broadcast([P, SLOTS, 2, DH // 2])
            copy(out=angle_twice[h][:], in_=words)

        def turn_angles(h, copy):
            bank = tr_psum.tile([P, SLOTS, P], F32, name="bank", tag="tr")
            for q in range(SLOTS):
                nc.tensor.transpose(bank[:, q, :], angle_twice[h][:, q].rearrange("p d j -> p (d j)"), ident[:])
            pairs = bank[:].rearrange("p q n -> p (q n)").bitcast(BF16).rearrange("p (n e) -> p e n", e=2)
            copy(out=table[h][:, 1:3, :], in_=pairs)

        sums, shifted, terms, addends = {}, {}, {}, {}

        def pool_products(i):
            g, u = divmod(i, UNITS)
            return P * by_group(g, FIRST_POOL_PRODUCTS, POOL_PRODUCTS, LAST_POOL_PRODUCTS)[u]

        def pool_sums(i):
            g, u = divmod(i, UNITS)
            return P * by_group(g, FIRST_POOL_SUMS, POOL_SUMS, LAST_POOL_SUMS)[u]

        def unit_bias(i, e):
            qk, pair = divmod(i % UNITS, 2)
            return bias[qk][:, pair, e : e + 1]

        def matmul(acc, i, e, cols):
            g, u = divmod(i, UNITS)
            features = slice(e * P, (e + 1) * P)
            nc.tensor.matmul_mx(
                out=acc,
                lhsT=w_codes[:, u, features].bitcast(E4M3X4),
                lhsT_scale=w_scales[:, u, features],
                rhs=x_codes[g][:, cols].bitcast(E5M2X4),
                rhs_scale=x_scales[g][:, cols],
                start=True,
                stop=True,
            )

        def project(i):
            sums[i] = []
            for e in range(2):
                acc = mx_psum.tile([P, GROUP], F32, name="acc")
                matmul(acc[:], i, e, slice(0, GROUP))
                sums[i].append(acc)
            n = pool_products(i)
            if n:
                shifted[i] = work.tile([P, n], F32, name="shifted")
                nc.scalar.activation(out=shifted[i][:], in_=sums[i][1][:, :n], func=ACT.Identity, bias=unit_bias(i, 1))

        def project_half(i, cols):
            acc = mx_psum.tile([P, 2, HALF], F32, name="acc")
            for e in range(2):
                matmul(acc[:, e, :], i, e, cols)
            return acc

        def new_terms(i):
            terms[i] = [prod.tile([P, 2, GROUP], F32, name="term%d" % e) for e in range(2)]

        def vector_products(i, e, acc, cols):
            nc.vector.scalar_tensor_tensor(
                out=terms[i][e][:, :, cols],
                in0=acc.unsqueeze(1).to_broadcast([P, 2, cols.stop - cols.start]),
                scalar=unit_bias(i, e),
                in1=table[i // UNITS // B][:, 1 - e : 3 - e, cols],
                op0=ALU.add,
                op1=ALU.mult,
            )

        def multiply(i):
            new_terms(i)
            width = P if i == LAST_UNIT else GROUP
            n = pool_products(i)
            for start in range(0, GROUP, width):
                vector_products(i, 0, sums[i][0][:, start : start + width], slice(start, start + width))
                if n < start + width:
                    cols = slice(max(n, start), start + width)
                    vector_products(i, 1, sums[i][1][:, cols], cols)
            if n:
                nc.gpsimd.tensor_tensor(
                    out=terms[i][1][:, :, :n],
                    in0=shifted[i][:].unsqueeze(1).to_broadcast([P, 2, n]),
                    in1=table[i // UNITS // B][:, 0:2, :n],
                    op=ALU.mult,
                )

        def combine(i):
            addends[i] = [terms[i]] * SLOTS
            n = pool_sums(i)
            if n:
                total = prod.tile([P, 2, n], F32, name="total", bufs=LAG + 2)
                nc.gpsimd.tensor_tensor(
                    out=total[:], in0=terms[i][0][:, :, :n], in1=terms[i][1][:, :, :n], op=ALU.add
                )
                addends[i] = [[total] if q * P < n else terms[i] for q in range(SLOTS)]

        def finish(i):
            g, u = divmod(i, UNITS)
            qk, pair = divmod(u, 2)
            hbm = out_rows[qk][group_rows(g), pair * 2 * DH : (pair + 1) * 2 * DH]
            hbm = hbm.rearrange("(p q) f -> p q f", q=SLOTS)
            per_bank = 1 if i == LAST_UNIT else 2
            for first in range(0, SLOTS, per_bank):
                bank = tr_psum.tile([P, per_bank, 2, 2, DH // 2], F32, name="bank", tag="tr")
                for q in range(first, first + per_bank):
                    for r in range(2):
                        for t, addend in enumerate(addends[i][q]):
                            nc.tensor.matmul(
                                out=bank[:, q - first, :, r, :],
                                lhsT=addend[:, r, q * P : (q + 1) * P],
                                rhs=ident[:],
                                start=(t == 0),
                                stop=(t == len(addends[i][q]) - 1),
                                is_transpose=True,
                            )
                rows = result.tile([P, per_bank, 2 * DH], F32, name="rows")
                nc.scalar.copy(out=rows[:], in_=bank[:].rearrange("p q h r j -> p q (h r j)"))
                nc.sync.dma_start(out=hbm[:, first : first + per_bank, :], in_=rows[:])

        zeros = keep.tile([P, GROUP], BF16, name="zeros")
        unread = mx_psum.tile([P, GROUP], F32, name="unread", tag="acc")
        nc.vector.memset(zeros[:], 0.0)

        def warm_up():
            nc.tensor.matmul(out=unread[:], lhsT=zeros[:, :P], rhs=zeros[:], start=True, stop=True)

        for step in range(WARM_UPS):
            warm_up()

        low, high = slice(0, HALF), slice(HALF, GROUP)
        repeat_angles(0, nc.vector.tensor_copy)
        turn_angles(0, nc.vector.tensor_copy)
        nc.vector.tensor_scalar_mul(out=table[0][:, 0, :], in0=table[0][:, 2, :], scalar1=-1.0)
        turn_w(0)
        turn_x(0, 0)
        quantize_w(slice(0, 1))
        quantize_x(0, low)
        turn_x(0, 1)
        warm_up()
        turn_w(1)
        acc_low = project_half(0, low)
        quantize_x(0, high)
        acc_high = project_half(0, high)
        for u in range(2, UNITS):
            turn_w(u)
        new_terms(0)
        for e in range(2):
            vector_products(0, e, acc_low[:, e, :], low)
        quantize_w(slice(1, 2))
        for e in range(2):
            vector_products(0, e, acc_high[:, e, :], high)
        quantize_w(slice(2, UNITS))

        for i in range(LAST_UNIT + LAG + 1):
            g, u = divmod(i, UNITS)
            if i < LAST_UNIT:
                project(i + 1)
            for part in range(2):
                ahead, rest = divmod(i + 2 - part, UNITS)
                if rest == 0 and DIRECT_GROUPS <= ahead + 1 < GROUPS:
                    split_x(ahead + 1, part)
            for part in range(2):
                ahead, rest = divmod(i + 1 - part, UNITS)
                if i == 0:
                    turn_x(1, part)
                elif rest == 0 and ahead + 1 < GROUPS:
                    turn_x(ahead + 1, part)
            if 0 < i <= LAST_UNIT:
                multiply(i)
            if i <= LAST_UNIT:
                combine(i)
            if g + 1 < GROUPS and u == (FIRST_QUANTIZE_AFTER if g == 0 else QUANTIZE_AFTER):
                quantize_x(g + 1, slice(0, GROUP))
            if i == SECOND_TABLE_STEP:
                repeat_angles(1, nc.scalar.copy)
            if i == SECOND_TABLE_STEP + 2:
                turn_angles(1, nc.scalar.copy)
                nc.scalar.mul(out=table[1][:, 0, :], in_=table[1][:, 2, :], mul=-1.0)
            if i >= LAG:
                finish(i - LAG)
